import numpy as np
import ml_dtypes


def mxq(x, axis, fmt="e4m3"):
    dtype, down = {"e4m3": (ml_dtypes.float8_e4m3fn, 7), "e5m2": (ml_dtypes.float8_e5m2, 14)}[fmt]
    v = np.moveaxis(np.asarray(x, np.float32).astype(ml_dtypes.bfloat16).astype(np.float64), axis, -1)
    blocks = v.reshape(v.shape[:-1] + (-1, 32))
    amax = np.abs(blocks).max(-1, keepdims=True)
    byte = np.maximum(np.where(amax > 0, np.frexp(amax)[1] - 1 + 127, 0) - down, 1)
    scale = np.exp2(byte - 127.0)
    codes = (blocks / scale).astype(np.float32).astype(dtype).astype(np.float64)
    return np.moveaxis((codes * scale).reshape(v.shape), -1, axis)


WIDE = False


def mx_kscale(k):
    if not WIDE:
        return np.ones(k)
    levels = np.array([10, -10, 5, -5, 0])
    a = np.random.permutation(np.resize(levels, k // 512 * 4)).reshape(k // 512, 4)
    idx = np.arange(k)
    return np.exp2(a[idx // 512, idx % 128 // 32])


BF16 = ml_dtypes.bfloat16


def bf(x):
    return np.asarray(x, np.float32).astype(BF16)


def f64(x):
    return np.asarray(x).astype(np.float64)


B, S, D, HQ, HK, HD = 2, 256, 2048, 16, 8, 128
QD = HQ * HD
KD = HK * HD
E = QD + 2 * KD
EPS = 1e-6
ROPE_BASE = 10000.0
QK_RMS = 0.003


def rope_tables():
    inv_freq = 1.0 / ROPE_BASE ** (np.arange(0, HD, 2) / HD)
    freqs = np.outer(np.arange(S), inv_freq)
    emb = np.concatenate([freqs, freqs], axis=-1)
    return np.cos(emb), np.sin(emb)


def rms_norm(h, w):
    var = np.mean(np.square(h), axis=-1, keepdims=True)
    return h * (1.0 / np.sqrt(var + EPS)) * w


def rotate_half(h):
    h1, h2 = np.split(h, 2, axis=-1)
    return np.concatenate([-h2, h1], axis=-1)


def apply_rope(h, cos, sin):
    return h * cos[None, :, None, :] + rotate_half(h) * sin[None, :, None, :]


def setup_inputs():
    s = mx_kscale(D)
    cos, sin = rope_tables()
    row = np.concatenate([np.full(QD + KD, QK_RMS), np.ones(KD)])
    return {"x": bf(np.random.standard_normal((B, S, D)) * s),
            "pos_cos": bf(cos),
            "pos_sin": bf(sin),
            "w_qkv": bf(np.random.standard_normal((E, D)) * row[:, None] / np.sqrt(D) / s[None, :]),
            "q_norm_w": bf(1.0 + 0.1 * np.random.standard_normal(HD)),
            "k_norm_w": bf(1.0 + 0.1 * np.random.standard_normal(HD))}


def reference(x, pos_cos, pos_sin, w_qkv, q_norm_w, k_norm_w):
    xq = mxq(f64(x), 2, "e4m3")
    wt = f64(w_qkv).T
    q = (xq @ mxq(wt[:, :QD], 0, "e4m3")).reshape(B, S, HQ, HD)
    k = (xq @ mxq(wt[:, QD:QD + KD], 0, "e4m3")).reshape(B, S, HK, HD)
    v = (xq @ mxq(wt[:, QD + KD:], 0, "e4m3")).reshape(B, S, HK, HD)
    cos, sin = f64(pos_cos), f64(pos_sin)
    q = apply_rope(rms_norm(q, f64(q_norm_w)), cos, sin)
    k = apply_rope(rms_norm(k, f64(k_norm_w)), cos, sin)
    return q, k, v

@@ -1,0 +1,254 @@
+from contextlib import ExitStack
+
+import concourse.mybir as mybir
+from concourse.masks import make_identity
+
+F32 = mybir.dt.float32
+BF16 = mybir.dt.bfloat16
+U32 = mybir.dt.uint32
+U8 = mybir.dt.uint8
+FP8X4 = mybir.dt.float8_e4m3fn_x4
+ACT = mybir.ActivationFunctionType
+ALU = mybir.AluOpType
+
+P = 128
+D_MODEL = 2048
+PASSES = 4
+HEAD = 128
+HALF = HEAD // 2
+ROWS = 512
+ROW_TILES = ROWS // P
+HEADS = ROWS // HEAD
+N_GROUPS = 8
+EPS = 1e-6
+
+LOADS_AHEAD = 4
+SHARED_SOURCES = 2
+LAG = 4
+
+FLOPS = 2 * 512 * 4096 * 2048
+
+
+def tile_qwen3attention_pa_kernel(
+    tc, x, pos_cos, pos_sin, w_qkv, q_norm_w, k_norm_w, out_0, out_1, out_2
+):
+    nc = tc.nc
+    with ExitStack() as ctx:
+        ctx.enter_context(tc.manual_schedule())
+        const = ctx.enter_context(tc.tile_pool(name="const", bufs=1))
+        raw_pool = ctx.enter_context(tc.tile_pool(name="raw", bufs=LOADS_AHEAD))
+        grouped_pool = ctx.enter_context(tc.tile_pool(name="grouped", bufs=4))
+        codes_pool = ctx.enter_context(tc.tile_pool(name="codes", bufs=3))
+        small = ctx.enter_context(tc.tile_pool(name="small", bufs=4))
+        scratch = ctx.enter_context(tc.tile_pool(name="scratch", bufs=2))
+        products_pool = ctx.enter_context(tc.tile_pool(name="products", bufs=4))
+        result_pool = ctx.enter_context(tc.tile_pool(name="result", bufs=8))
+        psum_t = ctx.enter_context(tc.psum_pool(name="psum_t", bufs=4))
+        psum_acc = ctx.enter_context(tc.psum_pool(name="psum_acc", bufs=4))
+
+        sources = [x.rearrange("b s d -> (b s) d")]
+        for g in range(N_GROUPS):
+            sources.append(w_qkv[g * ROWS : (g + 1) * ROWS, :])
+        raws = {}
+        codes = {}
+        scales = {}
+
+        def load(s):
+            raw = raw_pool.tile([P, ROW_TILES, D_MODEL], BF16)
+            nc.sync.dma_start(out=raw[:], in_=sources[s].rearrange("(r p) k -> p r k", p=P))
+            raws[s] = raw
+
+        load(0)
+        cos = const.tile([P, 2, HEAD], BF16)
+        sin = const.tile([P, 2, HEAD], BF16)
+        nc.sync.dma_start(out=cos[:], in_=pos_cos.rearrange("(t p) d -> p t d", p=P))
+        nc.sync.dma_start(out=sin[:], in_=pos_sin.rearrange("(t p) d -> p t d", p=P))
+        gain_rows = const.tile([P, 2, HEAD], BF16)
+        nc.vector.memset(gain_rows[:], 0.0)
+        nc.sync.dma_start(out=gain_rows[0:1, 0, :], in_=q_norm_w.rearrange("(o d) -> o d", o=1))
+        nc.sync.dma_start(out=gain_rows[0:1, 1, :], in_=k_norm_w.rearrange("(o d) -> o d", o=1))
+        for s in range(1, LOADS_AHEAD):
+            load(s)
+
+        ident = const.tile([P, P], F32)
+        make_identity(nc, ident[:])
+        eps = const.tile([P, 1], F32)
+        nc.vector.memset(eps[:], EPS)
+        warm = const.tile([P, 1], F32)
+        nc.scalar.activation(out=warm[:], in_=eps[:], func=ACT.Sqrt)
+
+        ones = const.tile([P, P], BF16)
+        nc.vector.memset(ones[:], 1.0)
+        acc = psum_acc.tile([P, ROWS], F32)
+        nc.tensor.matmul(
+            out=acc[:, 0 : 2 * HEAD],
+            lhsT=ones[:],
+            rhs=gain_rows[:].rearrange("p g d -> p (g d)"),
+            start=True,
+            stop=True,
+        )
+        gains = const.tile([P, 2, HEAD], F32)
+        nc.vector.tensor_copy(out=gains[:].rearrange("p g d -> p (g d)"), in_=acc[:, 0 : 2 * HEAD])
+
+        tables = []
+        for kind in range(2):
+            table = const.tile([P, 2, 2, HEAD], F32, name="table%d" % kind)
+            nc.gpsimd.tensor_tensor(
+                out=table[:, :, 0, :],
+                in0=cos[:],
+                in1=gains[:, kind, :].unsqueeze(1).to_broadcast([P, 2, HEAD]),
+                op=ALU.mult,
+            )
+            nc.gpsimd.tensor_tensor(
+                out=table[:, :, 1, 0:HALF],
+                in0=sin[:, :, HALF:HEAD],
+                in1=gains[:, kind, 0:HALF].unsqueeze(1).to_broadcast([P, 2, HALF]),
+                op=ALU.mult,
+            )
+            nc.gpsimd.tensor_tensor(
+                out=table[:, :, 1, HALF:HEAD],
+                in0=sin[:, :, 0:HALF],
+                in1=gains[:, kind, HALF:HEAD].unsqueeze(1).to_broadcast([P, 2, HALF]),
+                op=ALU.mult,
+            )
+            tables.append(table)
+
+        groups = []
+        for out, table in ((out_0, tables[0]), (out_1, tables[1]), (out_2, None)):
+            flat = out.rearrange("b s h d -> (b s) (h d)")
+            for col in range(0, flat.shape[1], ROWS):
+                groups.append((flat[:, col : col + ROWS], table))
+
+        def transpose_half(s, half):
+            if half == 0:
+                code_words = codes_pool.tile([P, PASSES, ROWS], U32, align_bytes=64)
+                scale_bytes = codes_pool.tile([P, PASSES, ROWS], U8, align_bytes=64)
+                codes[s] = code_words
+                scales[s] = scale_bytes
+            raw_words = raws[s][:].bitcast(F32)
+            made = []
+            for c in (2 * half, 2 * half + 1):
+                grouped = grouped_pool.tile([P, 4 * ROWS], BF16, align_bytes=64)
+                grouped_words = grouped[:].bitcast(F32).rearrange("p (n u) -> p n u", u=2)
+                for pair in range(ROW_TILES // 2):
+                    bank = psum_t.tile([P, 2, 2 * P], F32)
+                    for u in range(2):
+                        for rr in range(2):
+                            first = (2 * c + u) * P
+                            nc.tensor.transpose(
+                                bank[:, u, rr * P : (rr + 1) * P],
+                                raw_words[:, 2 * pair + rr, first : first + P],
+                                ident[:],
+                            )
+                    copy_out = nc.scalar.copy
+                    if s < SHARED_SOURCES and pair == 1:
+                        copy_out = nc.vector.tensor_copy
+                    copy_out(
+                        out=grouped_words[:, pair * 2 * P : (pair + 1) * 2 * P, :],
+                        in_=bank[:].rearrange("p u n -> p n u"),
+                    )
+                made.append((c, grouped))
+            return made
+
+        def quantise_half(s, made):
+            for c, grouped in made:
+                nc.vector.quantize_mx(
+                    out=codes[s][:, c, :].bitcast(FP8X4),
+                    scales=scales[s][:, c, :],
+                    in_=grouped[:],
+                )
+
+        def matmul_half(g, half):
+            sums = []
+            for m in (2 * half, 2 * half + 1):
+                acc = psum_acc.tile([P, ROWS], F32)
+                sums.append((m, acc))
+            for c in range(PASSES):
+                for m, acc in sums:
+                    nc.tensor.matmul_mx(
+                        out=acc[:],
+                        lhsT=codes[0][:, c, m * P : (m + 1) * P].bitcast(FP8X4),
+                        lhsT_scale=scales[0][:, c, m * P : (m + 1) * P],
+                        rhs=codes[g + 1][:, c, :].bitcast(FP8X4),
+                        rhs_scale=scales[g + 1][:, c, :],
+                        start=(c == 0),
+                        stop=(c == PASSES - 1),
+                    )
+            return sums
+
+        def norm_and_rope(g, sums):
+            dst, table = groups[g]
+            sumsq = small.tile([P, 2 * HEADS], F32)
+            squares = scratch.tile([P, 2 * HEADS, HEAD], BF16)
+            for b, (m, acc) in enumerate(sums):
+                for h in range(HEADS):
+                    nc.scalar.activation(
+                        out=squares[:, b * HEADS + h, :],
+                        in_=acc[:, h * HEAD : (h + 1) * HEAD],
+                        func=ACT.Square,
+                        accum_out=sumsq[:, b * HEADS + h : b * HEADS + h + 1],
+                    )
+            rms = small.tile([P, 2 * HEADS], F32)
+            nc.scalar.activation(
+                out=rms[:], in_=sumsq[:], func=ACT.Sqrt, scale=1.0 / HEAD, bias=eps[:, 0:1]
+            )
+            inv_rms = small.tile([P, 2 * HEADS], F32)
+            nc.vector.reciprocal(out=inv_rms[:], in_=rms[:])
+            for b, (m, acc) in enumerate(sums):
+                products = products_pool.tile([P, HEADS, 2, HEAD], F32)
+                for h in range(HEADS):
+                    nc.vector.scalar_tensor_tensor(
+                        out=products[:, h, :, :],
+                        in0=acc[:, h * HEAD : (h + 1) * HEAD].unsqueeze(1).to_broadcast([P, 2, HEAD]),
+                        scalar=inv_rms[:, b * HEADS + h : b * HEADS + h + 1],
+                        in1=table[:, m % 2, :, :],
+                        op0=ALU.mult,
+                        op1=ALU.mult,
+                    )
+                result = result_pool.tile([P, HEADS, HEAD], F32)
+                nc.gpsimd.tensor_tensor(
+                    out=result[:, :, 0:HALF],
+                    in0=products[:, :, 0, 0:HALF],
+                    in1=products[:, :, 1, HALF:HEAD],
+                    op=ALU.subtract,
+                )
+                nc.gpsimd.tensor_tensor(
+                    out=result[:, :, HALF:HEAD],
+                    in0=products[:, :, 0, HALF:HEAD],
+                    in1=products[:, :, 1, 0:HALF],
+                    op=ALU.add,
+                )
+                nc.sync.dma_start(
+                    out=dst[m * P : (m + 1) * P, :], in_=result[:].rearrange("p h d -> p (h d)")
+                )
+
+        def copy_values(g, sums):
+            dst, table = groups[g]
+            for b, (m, acc) in enumerate(sums):
+                result = result_pool.tile([P, HEADS, HEAD], F32)
+                flat = result[:].rearrange("p h d -> p (h d)")
+                if b == 0:
+                    nc.scalar.copy(out=flat, in_=acc[:])
+                else:
+                    nc.vector.tensor_copy(out=flat, in_=acc[:])
+                nc.sync.dma_start(out=dst[m * P : (m + 1) * P, :], in_=flat)
+
+        n_transposes = 2 * (N_GROUPS + 1)
+        n_matmuls = 2 * N_GROUPS
+        waiting = {}
+        for i in range(n_matmuls + LAG + 1):
+            j = i - LAG - 1
+            if 0 <= j < n_matmuls:
+                if groups[j // 2][1] is None:
+                    copy_values(j // 2, waiting[j])
+                else:
+                    norm_and_rope(j // 2, waiting[j])
+            made = []
+            if i < n_transposes:
+                made = transpose_half(i // 2, i % 2)
+                if i % 2 == 1 and i // 2 + LOADS_AHEAD <= N_GROUPS:
+                    load(i // 2 + LOADS_AHEAD)
+            j = i - LAG
+            if 0 <= j < n_matmuls:
+                waiting[j] = matmul_half(j // 2, j % 2)
+            quantise_half(i // 2, made)

@@ -41,7 +41,7 @@ def tile_qwen3attention_pa_kernel(
         codes_pool = ctx.enter_context(tc.tile_pool(name="codes", bufs=3))
         small = ctx.enter_context(tc.tile_pool(name="small", bufs=4))
         scratch = ctx.enter_context(tc.tile_pool(name="scratch", bufs=2))
-        products_pool = ctx.enter_context(tc.tile_pool(name="products", bufs=4))
+        products_pool = ctx.enter_context(tc.tile_pool(name="products", bufs=10))
         result_pool = ctx.enter_context(tc.tile_pool(name="result", bufs=8))
         psum_t = ctx.enter_context(tc.psum_pool(name="psum_t", bufs=4))
         psum_acc = ctx.enter_context(tc.psum_pool(name="psum_acc", bufs=4))

@@ -41,8 +41,8 @@ def tile_qwen3attention_pa_kernel(
         codes_pool = ctx.enter_context(tc.tile_pool(name="codes", bufs=3))
         small = ctx.enter_context(tc.tile_pool(name="small", bufs=4))
         scratch = ctx.enter_context(tc.tile_pool(name="scratch", bufs=2))
-        products_pool = ctx.enter_context(tc.tile_pool(name="products", bufs=10))
-        result_pool = ctx.enter_context(tc.tile_pool(name="result", bufs=8))
+        products_pool = ctx.enter_context(tc.tile_pool(name="products", bufs=5))
+        result_pool = ctx.enter_context(tc.tile_pool(name="result", bufs=5))
         psum_t = ctx.enter_context(tc.psum_pool(name="psum_t", bufs=4))
         psum_acc = ctx.enter_context(tc.psum_pool(name="psum_acc", bufs=4))
 
@@ -55,18 +55,21 @@ def tile_qwen3attention_pa_kernel(
 
         def load(s):
             raw = raw_pool.tile([P, ROW_TILES, D_MODEL], BF16)
-            nc.sync.dma_start(out=raw[:], in_=sources[s].rearrange("(r p) k -> p r k", p=P))
+            rows = sources[s].rearrange("(r p) k -> p r k", p=P)
+            for half in range(2):
+                features = slice(half * D_MODEL // 2, (half + 1) * D_MODEL // 2)
+                nc.sync.dma_start(out=raw[:, :, features], in_=rows[:, :, features])
             raws[s] = raw
 
+        gain_rows = const.tile([P, 2, HEAD], BF16)
+        nc.vector.memset(gain_rows[:], 0.0)
+        nc.sync.dma_start(out=gain_rows[0:1, 0, :], in_=q_norm_w.rearrange("(o d) -> o d", o=1))
+        nc.sync.dma_start(out=gain_rows[0:1, 1, :], in_=k_norm_w.rearrange("(o d) -> o d", o=1))
         load(0)
         cos = const.tile([P, 2, HEAD], BF16)
         sin = const.tile([P, 2, HEAD], BF16)
         nc.sync.dma_start(out=cos[:], in_=pos_cos.rearrange("(t p) d -> p t d", p=P))
         nc.sync.dma_start(out=sin[:], in_=pos_sin.rearrange("(t p) d -> p t d", p=P))
-        gain_rows = const.tile([P, 2, HEAD], BF16)
-        nc.vector.memset(gain_rows[:], 0.0)
-        nc.sync.dma_start(out=gain_rows[0:1, 0, :], in_=q_norm_w.rearrange("(o d) -> o d", o=1))
-        nc.sync.dma_start(out=gain_rows[0:1, 1, :], in_=k_norm_w.rearrange("(o d) -> o d", o=1))
         for s in range(1, LOADS_AHEAD):
             load(s)
 
@@ -121,8 +124,9 @@ def tile_qwen3attention_pa_kernel(
 
         def transpose_half(s, half):
             if half == 0:
-                code_words = codes_pool.tile([P, PASSES, ROWS], U32, align_bytes=64)
-                scale_bytes = codes_pool.tile([P, PASSES, ROWS], U8, align_bytes=64)
+                pool = const if s == 0 else codes_pool
+                code_words = pool.tile([P, PASSES, ROWS], U32, align_bytes=64)
+                scale_bytes = pool.tile([P, PASSES, ROWS], U8, align_bytes=64)
                 codes[s] = code_words
                 scales[s] = scale_bytes
             raw_words = raws[s][:].bitcast(F32)
@@ -176,6 +180,13 @@ def tile_qwen3attention_pa_kernel(
                     )
             return sums
 
+        def store(dst, sums, result):
+            first = sums[0][0] * P
+            nc.sync.dma_start(
+                out=dst[first : first + 2 * P, :].rearrange("(b p) f -> p b f", p=P),
+                in_=result[:].rearrange("p (b h) d -> p b (h d)", b=2),
+            )
+
         def norm_and_rope(g, sums):
             dst, table = groups[g]
             sumsq = small.tile([P, 2 * HEADS], F32)
@@ -194,44 +205,42 @@ def tile_qwen3attention_pa_kernel(
             )
             inv_rms = small.tile([P, 2 * HEADS], F32)
             nc.vector.reciprocal(out=inv_rms[:], in_=rms[:])
+            products = products_pool.tile([P, 2 * HEADS, 2, HEAD], F32)
             for b, (m, acc) in enumerate(sums):
-                products = products_pool.tile([P, HEADS, 2, HEAD], F32)
                 for h in range(HEADS):
                     nc.vector.scalar_tensor_tensor(
-                        out=products[:, h, :, :],
+                        out=products[:, b * HEADS + h, :, :],
                         in0=acc[:, h * HEAD : (h + 1) * HEAD].unsqueeze(1).to_broadcast([P, 2, HEAD]),
                         scalar=inv_rms[:, b * HEADS + h : b * HEADS + h + 1],
                         in1=table[:, m % 2, :, :],
                         op0=ALU.mult,
                         op1=ALU.mult,
                     )
-                result = result_pool.tile([P, HEADS, HEAD], F32)
-                nc.gpsimd.tensor_tensor(
-                    out=result[:, :, 0:HALF],
-                    in0=products[:, :, 0, 0:HALF],
-                    in1=products[:, :, 1, HALF:HEAD],
-                    op=ALU.subtract,
-                )
-                nc.gpsimd.tensor_tensor(
-                    out=result[:, :, HALF:HEAD],
-                    in0=products[:, :, 0, HALF:HEAD],
-                    in1=products[:, :, 1, 0:HALF],
-                    op=ALU.add,
-                )
-                nc.sync.dma_start(
-                    out=dst[m * P : (m + 1) * P, :], in_=result[:].rearrange("p h d -> p (h d)")
-                )
+            result = result_pool.tile([P, 2 * HEADS, HEAD], F32)
+            nc.gpsimd.tensor_tensor(
+                out=result[:, :, 0:HALF],
+                in0=products[:, :, 0, 0:HALF],
+                in1=products[:, :, 1, HALF:HEAD],
+                op=ALU.subtract,
+            )
+            nc.gpsimd.tensor_tensor(
+                out=result[:, :, HALF:HEAD],
+                in0=products[:, :, 0, HALF:HEAD],
+                in1=products[:, :, 1, 0:HALF],
+                op=ALU.add,
+            )
+            store(dst, sums, result)
 
         def copy_values(g, sums):
             dst, table = groups[g]
+            result = result_pool.tile([P, 2 * HEADS, HEAD], F32)
             for b, (m, acc) in enumerate(sums):
-                result = result_pool.tile([P, HEADS, HEAD], F32)
-                flat = result[:].rearrange("p h d -> p (h d)")
+                flat = result[:, b * HEADS : (b + 1) * HEADS, :].rearrange("p h d -> p (h d)")
                 if b == 0:
                     nc.scalar.copy(out=flat, in_=acc[:])
                 else:
                     nc.vector.tensor_copy(out=flat, in_=acc[:])
-                nc.sync.dma_start(out=dst[m * P : (m + 1) * P, :], in_=flat)
+            store(dst, sums, result)
 
         n_transposes = 2 * (N_GROUPS + 1)
         n_matmuls = 2 * N_GROUPS

@@ -180,9 +180,9 @@ def tile_qwen3attention_pa_kernel(
                     )
             return sums
 
-        def store(dst, sums, result):
+        def store(queue, dst, sums, result):
             first = sums[0][0] * P
-            nc.sync.dma_start(
+            queue.dma_start(
                 out=dst[first : first + 2 * P, :].rearrange("(b p) f -> p b f", p=P),
                 in_=result[:].rearrange("p (b h) d -> p b (h d)", b=2),
             )
@@ -229,18 +229,15 @@ def tile_qwen3attention_pa_kernel(
                 in1=products[:, :, 1, 0:HALF],
                 op=ALU.add,
             )
-            store(dst, sums, result)
+            store(nc.sync, dst, sums, result)
 
         def copy_values(g, sums):
             dst, table = groups[g]
             result = result_pool.tile([P, 2 * HEADS, HEAD], F32)
             for b, (m, acc) in enumerate(sums):
                 flat = result[:, b * HEADS : (b + 1) * HEADS, :].rearrange("p h d -> p (h d)")
-                if b == 0:
-                    nc.scalar.copy(out=flat, in_=acc[:])
-                else:
-                    nc.vector.tensor_copy(out=flat, in_=acc[:])
-            store(dst, sums, result)
+                nc.scalar.copy(out=flat, in_=acc[:])
+            store(nc.scalar, dst, sums, result)
 
         n_transposes = 2 * (N_GROUPS + 1)
         n_matmuls = 2 * N_GROUPS

from contextlib import ExitStack

import concourse.mybir as mybir
from concourse.masks import make_identity

F32 = mybir.dt.float32
BF16 = mybir.dt.bfloat16
U32 = mybir.dt.uint32
U8 = mybir.dt.uint8
FP8X4 = mybir.dt.float8_e4m3fn_x4
ACT = mybir.ActivationFunctionType
ALU = mybir.AluOpType

P = 128
D_MODEL = 2048
PASSES = 4
HEAD = 128
HALF = HEAD // 2
ROWS = 512
ROW_TILES = ROWS // P
HEADS = ROWS // HEAD
N_GROUPS = 8
EPS = 1e-6

LOADS_AHEAD = 4
SHARED_SOURCES = 2
LAG = 4

FLOPS = 2 * 512 * 4096 * 2048


def tile_qwen3attention_pa_kernel(
    tc, x, pos_cos, pos_sin, w_qkv, q_norm_w, k_norm_w, out_0, out_1, out_2
):
    nc = tc.nc
    with ExitStack() as ctx:
        ctx.enter_context(tc.manual_schedule())
        const = ctx.enter_context(tc.tile_pool(name="const", bufs=1))
        raw_pool = ctx.enter_context(tc.tile_pool(name="raw", bufs=LOADS_AHEAD))
        grouped_pool = ctx.enter_context(tc.tile_pool(name="grouped", bufs=4))
        codes_pool = ctx.enter_context(tc.tile_pool(name="codes", bufs=3))
        small = ctx.enter_context(tc.tile_pool(name="small", bufs=4))
        scratch = ctx.enter_context(tc.tile_pool(name="scratch", bufs=2))
        products_pool = ctx.enter_context(tc.tile_pool(name="products", bufs=5))
        result_pool = ctx.enter_context(tc.tile_pool(name="result", bufs=5))
        psum_t = ctx.enter_context(tc.psum_pool(name="psum_t", bufs=4))
        psum_acc = ctx.enter_context(tc.psum_pool(name="psum_acc", bufs=4))

        sources = [x.rearrange("b s d -> (b s) d")]
        for g in range(N_GROUPS):
            sources.append(w_qkv[g * ROWS : (g + 1) * ROWS, :])
        raws = {}
        codes = {}
        scales = {}

        def load(s):
            raw = raw_pool.tile([P, ROW_TILES, D_MODEL], BF16)
            rows = sources[s].rearrange("(r p) k -> p r k", p=P)
            for half in range(2):
                features = slice(half * D_MODEL // 2, (half + 1) * D_MODEL // 2)
                nc.sync.dma_start(out=raw[:, :, features], in_=rows[:, :, features])
            raws[s] = raw

        gain_rows = const.tile([P, 2, HEAD], BF16)
        nc.vector.memset(gain_rows[:], 0.0)
        nc.sync.dma_start(out=gain_rows[0:1, 0, :], in_=q_norm_w.rearrange("(o d) -> o d", o=1))
        nc.sync.dma_start(out=gain_rows[0:1, 1, :], in_=k_norm_w.rearrange("(o d) -> o d", o=1))
        load(0)
        cos = const.tile([P, 2, HEAD], BF16)
        sin = const.tile([P, 2, HEAD], BF16)
        nc.sync.dma_start(out=cos[:], in_=pos_cos.rearrange("(t p) d -> p t d", p=P))
        nc.sync.dma_start(out=sin[:], in_=pos_sin.rearrange("(t p) d -> p t d", p=P))
        for s in range(1, LOADS_AHEAD):
            load(s)

        ident = const.tile([P, P], F32)
        make_identity(nc, ident[:])
        eps = const.tile([P, 1], F32)
        nc.vector.memset(eps[:], EPS)
        warm = const.tile([P, 1], F32)
        nc.scalar.activation(out=warm[:], in_=eps[:], func=ACT.Sqrt)

        ones = const.tile([P, P], BF16)
        nc.vector.memset(ones[:], 1.0)
        acc = psum_acc.tile([P, ROWS], F32)
        nc.tensor.matmul(
            out=acc[:, 0 : 2 * HEAD],
            lhsT=ones[:],
            rhs=gain_rows[:].rearrange("p g d -> p (g d)"),
            start=True,
            stop=True,
        )
        gains = const.tile([P, 2, HEAD], F32)
        nc.vector.tensor_copy(out=gains[:].rearrange("p g d -> p (g d)"), in_=acc[:, 0 : 2 * HEAD])

        tables = []
        for kind in range(2):
            table = const.tile([P, 2, 2, HEAD], F32, name="table%d" % kind)
            nc.gpsimd.tensor_tensor(
                out=table[:, :, 0, :],
                in0=cos[:],
                in1=gains[:, kind, :].unsqueeze(1).to_broadcast([P, 2, HEAD]),
                op=ALU.mult,
            )
            nc.gpsimd.tensor_tensor(
                out=table[:, :, 1, 0:HALF],
                in0=sin[:, :, HALF:HEAD],
                in1=gains[:, kind, 0:HALF].unsqueeze(1).to_broadcast([P, 2, HALF]),
                op=ALU.mult,
            )
            nc.gpsimd.tensor_tensor(
                out=table[:, :, 1, HALF:HEAD],
                in0=sin[:, :, 0:HALF],
                in1=gains[:, kind, HALF:HEAD].unsqueeze(1).to_broadcast([P, 2, HALF]),
                op=ALU.mult,
            )
            tables.append(table)

        groups = []
        for out, table in ((out_0, tables[0]), (out_1, tables[1]), (out_2, None)):
            flat = out.rearrange("b s h d -> (b s) (h d)")
            for col in range(0, flat.shape[1], ROWS):
                groups.append((flat[:, col : col + ROWS], table))

        def transpose_half(s, half):
            if half == 0:
                pool = const if s == 0 else codes_pool
                code_words = pool.tile([P, PASSES, ROWS], U32, align_bytes=64)
                scale_bytes = pool.tile([P, PASSES, ROWS], U8, align_bytes=64)
                codes[s] = code_words
                scales[s] = scale_bytes
            raw_words = raws[s][:].bitcast(F32)
            made = []
            for c in (2 * half, 2 * half + 1):
                grouped = grouped_pool.tile([P, 4 * ROWS], BF16, align_bytes=64)
                grouped_words = grouped[:].bitcast(F32).rearrange("p (n u) -> p n u", u=2)
                for pair in range(ROW_TILES // 2):
                    bank = psum_t.tile([P, 2, 2 * P], F32)
                    for u in range(2):
                        for rr in range(2):
                            first = (2 * c + u) * P
                            nc.tensor.transpose(
                                bank[:, u, rr * P : (rr + 1) * P],
                                raw_words[:, 2 * pair + rr, first : first + P],
                                ident[:],
                            )
                    copy_out = nc.scalar.copy
                    if s < SHARED_SOURCES and pair == 1:
                        copy_out = nc.vector.tensor_copy
                    copy_out(
                        out=grouped_words[:, pair * 2 * P : (pair + 1) * 2 * P, :],
                        in_=bank[:].rearrange("p u n -> p n u"),
                    )
                made.append((c, grouped))
            return made

        def quantise_half(s, made):
            for c, grouped in made:
                nc.vector.quantize_mx(
                    out=codes[s][:, c, :].bitcast(FP8X4),
                    scales=scales[s][:, c, :],
                    in_=grouped[:],
                )

        def matmul_half(g, half):
            sums = []
            for m in (2 * half, 2 * half + 1):
                acc = psum_acc.tile([P, ROWS], F32)
                sums.append((m, acc))
            for c in range(PASSES):
                for m, acc in sums:
                    nc.tensor.matmul_mx(
                        out=acc[:],
                        lhsT=codes[0][:, c, m * P : (m + 1) * P].bitcast(FP8X4),
                        lhsT_scale=scales[0][:, c, m * P : (m + 1) * P],
                        rhs=codes[g + 1][:, c, :].bitcast(FP8X4),
                        rhs_scale=scales[g + 1][:, c, :],
                        start=(c == 0),
                        stop=(c == PASSES - 1),
                    )
            return sums

        def store(queue, dst, sums, result):
            first = sums[0][0] * P
            queue.dma_start(
                out=dst[first : first + 2 * P, :].rearrange("(b p) f -> p b f", p=P),
                in_=result[:].rearrange("p (b h) d -> p b (h d)", b=2),
            )

        def norm_and_rope(g, sums):
            dst, table = groups[g]
            sumsq = small.tile([P, 2 * HEADS], F32)
            squares = scratch.tile([P, 2 * HEADS, HEAD], BF16)
            for b, (m, acc) in enumerate(sums):
                for h in range(HEADS):
                    nc.scalar.activation(
                        out=squares[:, b * HEADS + h, :],
                        in_=acc[:, h * HEAD : (h + 1) * HEAD],
                        func=ACT.Square,
                        accum_out=sumsq[:, b * HEADS + h : b * HEADS + h + 1],
                    )
            rms = small.tile([P, 2 * HEADS], F32)
            nc.scalar.activation(
                out=rms[:], in_=sumsq[:], func=ACT.Sqrt, scale=1.0 / HEAD, bias=eps[:, 0:1]
            )
            inv_rms = small.tile([P, 2 * HEADS], F32)
            nc.vector.reciprocal(out=inv_rms[:], in_=rms[:])
            products = products_pool.tile([P, 2 * HEADS, 2, HEAD], F32)
            for b, (m, acc) in enumerate(sums):
                for h in range(HEADS):
                    nc.vector.scalar_tensor_tensor(
                        out=products[:, b * HEADS + h, :, :],
                        in0=acc[:, h * HEAD : (h + 1) * HEAD].unsqueeze(1).to_broadcast([P, 2, HEAD]),
                        scalar=inv_rms[:, b * HEADS + h : b * HEADS + h + 1],
                        in1=table[:, m % 2, :, :],
                        op0=ALU.mult,
                        op1=ALU.mult,
                    )
            result = result_pool.tile([P, 2 * HEADS, HEAD], F32)
            nc.gpsimd.tensor_tensor(
                out=result[:, :, 0:HALF],
                in0=products[:, :, 0, 0:HALF],
                in1=products[:, :, 1, HALF:HEAD],
                op=ALU.subtract,
            )
            nc.gpsimd.tensor_tensor(
                out=result[:, :, HALF:HEAD],
                in0=products[:, :, 0, HALF:HEAD],
                in1=products[:, :, 1, 0:HALF],
                op=ALU.add,
            )
            store(nc.sync, dst, sums, result)

        def copy_values(g, sums):
            dst, table = groups[g]
            result = result_pool.tile([P, 2 * HEADS, HEAD], F32)
            for b, (m, acc) in enumerate(sums):
                flat = result[:, b * HEADS : (b + 1) * HEADS, :].rearrange("p h d -> p (h d)")
                nc.scalar.copy(out=flat, in_=acc[:])
            store(nc.scalar, dst, sums, result)

        n_transposes = 2 * (N_GROUPS + 1)
        n_matmuls = 2 * N_GROUPS
        waiting = {}
        for i in range(n_matmuls + LAG + 1):
            j = i - LAG - 1
            if 0 <= j < n_matmuls:
                if groups[j // 2][1] is None:
                    copy_values(j // 2, waiting[j])
                else:
                    norm_and_rope(j // 2, waiting[j])
            made = []
            if i < n_transposes:
                made = transpose_half(i // 2, i % 2)
                if i % 2 == 1 and i // 2 + LOADS_AHEAD <= N_GROUPS:
                    load(i // 2 + LOADS_AHEAD)
            j = i - LAG
            if 0 <= j < n_matmuls:
                waiting[j] = matmul_half(j // 2, j % 2)
            quantise_half(i // 2, made)
